import numpy as np
import ml_dtypes


def mxq(x, axis, fmt="e4m3"):
    dtype, down = {"e4m3": (ml_dtypes.float8_e4m3fn, 7), "e5m2": (ml_dtypes.float8_e5m2, 14)}[fmt]
    v = np.moveaxis(np.asarray(x, np.float32).astype(ml_dtypes.bfloat16).astype(np.float64), axis, -1)
    blocks = v.reshape(v.shape[:-1] + (-1, 32))
    amax = np.abs(blocks).max(-1, keepdims=True)
    byte = np.maximum(np.where(amax > 0, np.frexp(amax)[1] - 1 + 127, 0) - down, 1)
    scale = np.exp2(byte - 127.0)
    codes = (blocks / scale).astype(np.float32).astype(dtype).astype(np.float64)
    return np.moveaxis((codes * scale).reshape(v.shape), -1, axis)


WIDE = False


def mx_kscale(k):
    if not WIDE:
        return np.ones(k)
    levels = np.array([10, -10, 5, -5, 0])
    a = np.random.permutation(np.resize(levels, k // 512 * 4)).reshape(k // 512, 4)
    idx = np.arange(k)
    return np.exp2(a[idx // 512, idx % 128 // 32])


BF16 = ml_dtypes.bfloat16


def bf(x):
    return np.asarray(x, np.float32).astype(BF16)


def f64(x):
    return np.asarray(x).astype(np.float64)


B, S, HID, H, HKV, D, QB = 4, 2048, 1024, 2, 2, 64, 512
HALF = D // 2
ROPE_BASE = 10000.0


def rope_tables():
    inv_freq = 1.0 / (ROPE_BASE ** (np.arange(0, D, 2) / D))
    freqs = np.outer(np.arange(S), inv_freq)
    emb = np.concatenate([freqs, freqs], axis=-1)
    return np.cos(emb), np.sin(emb)


def rotate_half(t):
    return np.concatenate([-t[..., HALF:], t[..., :HALF]], axis=-1)


def apply_rope(t, cos, sin):
    return t * cos[None, None, :, :] + rotate_half(t) * sin[None, None, :, :]


def heads(y, n):
    return y.reshape(B, S, n, D).transpose(0, 2, 1, 3)


def setup_inputs():
    s = mx_kscale(HID)
    w = 1.0 / np.sqrt(HID)
    cos, sin = rope_tables()
    return {"x": bf(np.random.standard_normal((B, S, HID)) * s),
            "Wq": bf(np.random.standard_normal((H * D, HID)) * w / s[None, :]),
            "Wk": bf(np.random.standard_normal((HKV * D, HID)) * w / s[None, :]),
            "Wv": bf(np.random.standard_normal((HKV * D, HID)) * w / s[None, :]),
            "cos": bf(cos), "sin": bf(sin)}


def reference(x, Wq, Wk, Wv, cos, sin):
    xq = mxq(f64(x), 2, "e4m3")
    q = heads(xq @ mxq(f64(Wq), 1, "e4m3").T, H)
    k = heads(xq @ mxq(f64(Wk), 1, "e4m3").T, HKV)
    v = heads(xq @ mxq(f64(Wv), 1, "e4m3").T, HKV)
    c, sn = f64(cos), f64(sin)
    return apply_rope(q, c, sn), apply_rope(k, c, sn), v

@@ -1,0 +1,212 @@
+from contextlib import ExitStack
+
+import concourse.masks as masks
+import concourse.mybir as mybir
+
+F32 = mybir.dt.float32
+BF16 = mybir.dt.bfloat16
+U32 = mybir.dt.uint32
+U8 = mybir.dt.uint8
+FP8X4 = mybir.dt.float8_e4m3fn_x4
+MULT = mybir.AluOpType.mult
+ADD = mybir.AluOpType.add
+
+P = 128
+B, S, HID = 4, 2048, 1024
+HEADS, D = 2, 64
+HALF = D // 2
+GROUPS = 2 * HEADS
+
+K_PASS = 512
+PASSES = HID // K_PASS
+WORDS = HID // 2
+
+TILES = S // P
+CHUNK = 4
+CHUNKS_PER_BATCH = TILES // CHUNK
+NCHUNKS = B * CHUNKS_PER_BATCH
+
+PREFETCH = 4
+X_BUFS = 8
+
+LO, HI, V = 0, 1, 2
+
+FLOPS = 2 * B * S * HID * 3 * HEADS * D
+
+
+def tile_selfmha_pa_t_kernel(tc, x, Wq, Wk, Wv, cos, sin, out_0, out_1, out_2):
+    nc = tc.nc
+    with ExitStack() as ctx:
+        const = ctx.enter_context(tc.tile_pool(name="const", bufs=1))
+        xpool = ctx.enter_context(tc.tile_pool(name="xpool", bufs=X_BUFS))
+        quant = ctx.enter_context(tc.tile_pool(name="quant", bufs=3))
+        outs = ctx.enter_context(tc.tile_pool(name="outs", bufs=3))
+        psum = ctx.enter_context(tc.psum_pool(name="psum", bufs=1))
+        ctx.enter_context(tc.manual_schedule())
+
+        w_raw = []
+        for n, w in enumerate((Wq, Wk, Wv)):
+            w_sb = const.tile([P, HID], BF16, name="w_raw%d" % n)
+            nc.sync.dma_start(out=w_sb[:], in_=w)
+            w_raw.append(w_sb)
+
+        cos_sb = const.tile([P, TILES, D], BF16, name="cos_sb")
+        sin_sb = const.tile([P, TILES, D], BF16, name="sin_sb")
+        x_sb = {}
+
+        def load_chunk(c):
+            b, cb = divmod(c, CHUNKS_PER_BATCH)
+            x_sb[c] = xpool.tile([P, CHUNK * HID], BF16, name="x_c")
+            rows = x[b].rearrange("(p j) k -> p (j k)", j=TILES)
+            nc.sync.dma_start(
+                out=x_sb[c][:], in_=rows[:, cb * CHUNK * HID : (cb + 1) * CHUNK * HID]
+            )
+
+        load_chunk(0)
+        load_chunk(1)
+        nc.sync.dma_start(out=cos_sb[:], in_=cos.rearrange("(p j) d -> p j d", j=TILES))
+        nc.sync.dma_start(out=sin_sb[:], in_=sin.rearrange("(p j) d -> p j d", j=TILES))
+        for c in range(2, PREFETCH):
+            load_chunk(c)
+
+        ident = const.tile([P, P], F32, name="ident")
+        masks.make_identity(nc, ident[:])
+        nc.gpsimd.tensor_scalar_mul(out=sin_sb[:, :, 0:HALF], in0=sin_sb[:, :, 0:HALF], scalar1=-1.0)
+
+        def transpose_words(words):
+            bank = psum.tile([P, WORDS], F32, name="bank", tag="bank", bufs=3)
+            for blk in range(WORDS // P):
+                cols = slice(blk * P, (blk + 1) * P)
+                nc.tensor.transpose(bank[:, cols], words[:, cols], ident[:])
+            return bank
+
+        def by_pass(bank):
+            return bank[:].rearrange("p (g u r) -> p g r u", g=PASSES, u=2)
+
+        w_grouped = const.tile([P, 3 * PASSES * P * 4], BF16, name="w_grouped", align_bytes=64)
+        w_codes = const.tile([P, 3 * PASSES * P], U32, name="w_codes", align_bytes=64)
+        w_scales = const.tile([P, 3 * PASSES * P], U8, name="w_scales", align_bytes=64)
+        w_words = w_grouped[:].bitcast(F32).rearrange(
+            "p (t g c u) -> p t g c u", t=3, g=PASSES, u=2
+        )
+        for n in range(2):
+            bank = transpose_words(w_raw[n][:].bitcast(F32))
+            halves = bank[:].rearrange(
+                "p (g u h f i) -> p g f h i u", g=PASSES, u=2, h=HEADS, f=2
+            )
+            for g in range(PASSES):
+                for f in (LO, HI):
+                    dst = w_words[:, f, g, n * HEADS * HALF : (n + 1) * HEADS * HALF, :]
+                    nc.vector.tensor_copy(
+                        out=dst.rearrange("p (h i) u -> p h i u", h=HEADS), in_=halves[:, g, f]
+                    )
+        bank = transpose_words(w_raw[2][:].bitcast(F32))
+        nc.vector.tensor_copy(out=w_words[:, V], in_=by_pass(bank))
+        for t in range(3):
+            nc.vector.quantize_mx(
+                out=w_codes[:, t * PASSES * P : (t + 1) * PASSES * P].bitcast(FP8X4),
+                scales=w_scales[:, t * PASSES * P : (t + 1) * PASSES * P],
+                in_=w_grouped[:, t * PASSES * P * 4 : (t + 1) * PASSES * P * 4],
+            )
+
+        grouped = {}
+        codes = {}
+        scales = {}
+        sums = {}
+        qk_out = {}
+        rot = {}
+
+        def transpose_chunk(c):
+            grouped[c] = quant.tile([P, CHUNK * HID], BF16, name="grouped", align_bytes=64)
+            x_words = x_sb[c][:].bitcast(F32)
+            g_words = grouped[c][:].bitcast(F32)
+            for j in range(CHUNK):
+                cols = slice(j * WORDS, (j + 1) * WORDS)
+                bank = transpose_words(x_words[:, cols])
+                nc.scalar.copy(
+                    out=g_words[:, cols].rearrange("p (g r u) -> p g r u", g=PASSES, u=2),
+                    in_=by_pass(bank),
+                )
+
+        def quantise_chunk(c):
+            codes[c] = quant.tile([P, CHUNK * PASSES * P], U32, name="codes", align_bytes=64)
+            scales[c] = quant.tile([P, CHUNK * PASSES * P], U8, name="scales", align_bytes=64)
+            nc.vector.quantize_mx(
+                out=codes[c][:].bitcast(FP8X4), scales=scales[c][:], in_=grouped[c][:]
+            )
+
+        def multiply_chunk(c):
+            lo = psum.tile([P, CHUNK * P], F32, name="lo", tag="lo", bufs=2)
+            hi = psum.tile([P, CHUNK * P], F32, name="hi", tag="hi", bufs=2)
+            vv = psum.tile([P, CHUNK * P], F32, name="vv", tag="vv", bufs=1)
+            sums[c] = (lo, hi, vv)
+            for j in range(CHUNK):
+                for t in range(3):
+                    for g in range(PASSES):
+                        xc = slice((j * PASSES + g) * P, (j * PASSES + g + 1) * P)
+                        wc = slice((t * PASSES + g) * P, (t * PASSES + g + 1) * P)
+                        nc.tensor.matmul_mx(
+                            out=sums[c][t][:, j * P : (j + 1) * P],
+                            lhsT=codes[c][:, xc].bitcast(FP8X4),
+                            lhsT_scale=scales[c][:, xc],
+                            rhs=w_codes[:, wc].bitcast(FP8X4),
+                            rhs_scale=w_scales[:, wc],
+                            start=(g == 0),
+                            stop=(g == PASSES - 1),
+                        )
+
+        def out_rows(out_n, c):
+            b, cb = divmod(c, CHUNKS_PER_BATCH)
+            rows = out_n[b].rearrange("h (p j) d -> p h (j d)", j=TILES)
+            return rows[:, :, cb * CHUNK * D : (cb + 1) * CHUNK * D]
+
+        def store_v(c):
+            v_out = outs.tile([P, HEADS, CHUNK, D], F32, name="v_out")
+            nc.scalar.copy(
+                out=v_out[:].rearrange("p h j d -> p j h d"),
+                in_=sums[c][V][:].rearrange("p (j h d) -> p j h d", j=CHUNK, h=HEADS),
+            )
+            nc.sync.dma_start(out=out_rows(out_2, c), in_=v_out[:].rearrange("p h j d -> p h (j d)"))
+
+        def table(tab, c, f):
+            cb = c % CHUNKS_PER_BATCH
+            rows = tab[:, cb * CHUNK : (cb + 1) * CHUNK, f * HALF : (f + 1) * HALF]
+            return rows.unsqueeze(2).to_broadcast([P, CHUNK, GROUPS, HALF])
+
+        def rope_products(c):
+            qk_out[c] = outs.tile([P, GROUPS, CHUNK, D], F32, name="qk_out")
+            rot[c] = outs.tile([P, GROUPS, CHUNK, D], F32, name="rot")
+            for f in (LO, HI):
+                cols = slice(f * HALF, (f + 1) * HALF)
+                same = sums[c][f][:].rearrange("p (j g i) -> p j g i", j=CHUNK, g=GROUPS)
+                other = sums[c][1 - f][:].rearrange("p (j g i) -> p j g i", j=CHUNK, g=GROUPS)
+                nc.vector.tensor_tensor(
+                    out=qk_out[c][:, :, :, cols].rearrange("p g j i -> p j g i"),
+                    in0=same, in1=table(cos_sb, c, f), op=MULT,
+                )
+                nc.vector.tensor_tensor(
+                    out=rot[c][:, :, :, cols].rearrange("p g j i -> p j g i"),
+                    in0=other, in1=table(sin_sb, c, f), op=MULT,
+                )
+
+        def rope_sum_and_store(c):
+            nc.vector.tensor_tensor(out=qk_out[c][:], in0=qk_out[c][:], in1=rot[c][:], op=ADD)
+            for n, out_n in enumerate((out_0, out_1)):
+                nc.sync.dma_start(
+                    out=out_rows(out_n, c),
+                    in_=qk_out[c][:, n * HEADS : (n + 1) * HEADS].rearrange("p h j d -> p h (j d)"),
+                )
+
+        for s in range(-3, NCHUNKS):
+            if s + 3 + PREFETCH < NCHUNKS:
+                load_chunk(s + 3 + PREFETCH)
+            if s + 3 < NCHUNKS:
+                transpose_chunk(s + 3)
+            if s >= 0:
+                rope_products(s)
+            if 0 <= s + 2 < NCHUNKS:
+                quantise_chunk(s + 2)
+                multiply_chunk(s + 2)
+                store_v(s + 2)
+            if s >= 0:
+                rope_sum_and_store(s)

@@ -190,7 +190,7 @@ def tile_selfmha_pa_t_kernel(tc, x, Wq, Wk, Wv, cos, sin, out_0, out_1, out_2):
                 )
 
         def rope_sum_and_store(c):
-            nc.vector.tensor_tensor(out=qk_out[c][:], in0=qk_out[c][:], in1=rot[c][:], op=ADD)
+            nc.gpsimd.tensor_tensor(out=qk_out[c][:], in0=qk_out[c][:], in1=rot[c][:], op=ADD)
             for n, out_n in enumerate((out_0, out_1)):
                 nc.sync.dma_start(
                     out=out_rows(out_n, c),

@@ -27,6 +27,7 @@ CHUNKS_PER_BATCH = TILES // CHUNK
 NCHUNKS = B * CHUNKS_PER_BATCH
 
 PREFETCH = 4
+OUT_BUFS = 6
 X_BUFS = 8
 
 LO, HI, V = 0, 1, 2
@@ -40,7 +41,7 @@ def tile_selfmha_pa_t_kernel(tc, x, Wq, Wk, Wv, cos, sin, out_0, out_1, out_2):
         const = ctx.enter_context(tc.tile_pool(name="const", bufs=1))
         xpool = ctx.enter_context(tc.tile_pool(name="xpool", bufs=X_BUFS))
         quant = ctx.enter_context(tc.tile_pool(name="quant", bufs=3))
-        outs = ctx.enter_context(tc.tile_pool(name="outs", bufs=3))
+        outs = ctx.enter_context(tc.tile_pool(name="outs", bufs=OUT_BUFS))
         psum = ctx.enter_context(tc.psum_pool(name="psum", bufs=1))
         ctx.enter_context(tc.manual_schedule())
 

@@ -23,10 +23,12 @@ WORDS = HID // 2
 
 TILES = S // P
 CHUNK = 4
+RUN = 2
+RUNS = CHUNK // RUN
 CHUNKS_PER_BATCH = TILES // CHUNK
 NCHUNKS = B * CHUNKS_PER_BATCH
 
-PREFETCH = 4
+PREFETCH = 7
 OUT_BUFS = 6
 X_BUFS = 8
 
@@ -117,11 +119,12 @@ def tile_selfmha_pa_t_kernel(tc, x, Wq, Wk, Wv, cos, sin, out_0, out_1, out_2):
         qk_out = {}
         rot = {}
 
-        def transpose_chunk(c):
-            grouped[c] = quant.tile([P, CHUNK * HID], BF16, name="grouped", align_bytes=64)
+        def transpose_run(c, r):
+            if r == 0:
+                grouped[c] = quant.tile([P, CHUNK * HID], BF16, name="grouped", align_bytes=64)
             x_words = x_sb[c][:].bitcast(F32)
             g_words = grouped[c][:].bitcast(F32)
-            for j in range(CHUNK):
+            for j in range(r * RUN, (r + 1) * RUN):
                 cols = slice(j * WORDS, (j + 1) * WORDS)
                 bank = transpose_words(x_words[:, cols])
                 nc.scalar.copy(
@@ -132,16 +135,21 @@ def tile_selfmha_pa_t_kernel(tc, x, Wq, Wk, Wv, cos, sin, out_0, out_1, out_2):
         def quantise_chunk(c):
             codes[c] = quant.tile([P, CHUNK * PASSES * P], U32, name="codes", align_bytes=64)
             scales[c] = quant.tile([P, CHUNK * PASSES * P], U8, name="scales", align_bytes=64)
-            nc.vector.quantize_mx(
-                out=codes[c][:].bitcast(FP8X4), scales=scales[c][:], in_=grouped[c][:]
-            )
+            for r in range(RUNS):
+                cols = slice(r * RUN * PASSES * P, (r + 1) * RUN * PASSES * P)
+                nc.vector.quantize_mx(
+                    out=codes[c][:, cols].bitcast(FP8X4),
+                    scales=scales[c][:, cols],
+                    in_=grouped[c][:, r * RUN * HID : (r + 1) * RUN * HID],
+                )
 
-        def multiply_chunk(c):
-            lo = psum.tile([P, CHUNK * P], F32, name="lo", tag="lo", bufs=2)
-            hi = psum.tile([P, CHUNK * P], F32, name="hi", tag="hi", bufs=2)
-            vv = psum.tile([P, CHUNK * P], F32, name="vv", tag="vv", bufs=1)
-            sums[c] = (lo, hi, vv)
-            for j in range(CHUNK):
+        def multiply_run(c, r):
+            if r == 0:
+                lo = psum.tile([P, CHUNK * P], F32, name="lo", tag="lo", bufs=2)
+                hi = psum.tile([P, CHUNK * P], F32, name="hi", tag="hi", bufs=2)
+                vv = psum.tile([P, CHUNK * P], F32, name="vv", tag="vv", bufs=1)
+                sums[c] = (lo, hi, vv)
+            for j in range(r * RUN, (r + 1) * RUN):
                 for t in range(3):
                     for g in range(PASSES):
                         xc = slice((j * PASSES + g) * P, (j * PASSES + g + 1) * P)
@@ -191,7 +199,8 @@ def tile_selfmha_pa_t_kernel(tc, x, Wq, Wk, Wv, cos, sin, out_0, out_1, out_2):
                 )
 
         def rope_sum_and_store(c):
-            nc.gpsimd.tensor_tensor(out=qk_out[c][:], in0=qk_out[c][:], in1=rot[c][:], op=ADD)
+            adder = nc.vector if c == NCHUNKS - 1 else nc.gpsimd
+            adder.tensor_tensor(out=qk_out[c][:], in0=qk_out[c][:], in1=rot[c][:], op=ADD)
             for n, out_n in enumerate((out_0, out_1)):
                 nc.sync.dma_start(
                     out=out_rows(out_n, c),
@@ -201,13 +210,16 @@ def tile_selfmha_pa_t_kernel(tc, x, Wq, Wk, Wv, cos, sin, out_0, out_1, out_2):
         for s in range(-3, NCHUNKS):
             if s + 3 + PREFETCH < NCHUNKS:
                 load_chunk(s + 3 + PREFETCH)
-            if s + 3 < NCHUNKS:
-                transpose_chunk(s + 3)
             if s >= 0:
                 rope_products(s)
             if 0 <= s + 2 < NCHUNKS:
                 quantise_chunk(s + 2)
-                multiply_chunk(s + 2)
+            for r in range(RUNS):
+                if s + 3 < NCHUNKS:
+                    transpose_run(s + 3, r)
+                if 0 <= s + 2 < NCHUNKS:
+                    multiply_run(s + 2, r)
+            if 0 <= s + 2 < NCHUNKS:
                 store_v(s + 2)
             if s >= 0:
                 rope_sum_and_store(s)

@@ -17,9 +17,10 @@ HEADS, D = 2, 64
 HALF = D // 2
 GROUPS = 2 * HEADS
 
-K_PASS = 512
+K_PASS = 4 * P
 PASSES = HID // K_PASS
 WORDS = HID // 2
+BLOCKS = WORDS // P
 
 TILES = S // P
 CHUNK = 4
@@ -28,9 +29,9 @@ RUNS = CHUNK // RUN
 CHUNKS_PER_BATCH = TILES // CHUNK
 NCHUNKS = B * CHUNKS_PER_BATCH
 
-PREFETCH = 7
-OUT_BUFS = 6
 X_BUFS = 8
+PREFETCH = X_BUFS - 1
+OUT_BUFS = 3
 
 LO, HI, V = 0, 1, 2
 
@@ -53,24 +54,27 @@ def tile_selfmha_pa_t_kernel(tc, x, Wq, Wk, Wv, cos, sin, out_0, out_1, out_2):
             nc.sync.dma_start(out=w_sb[:], in_=w)
             w_raw.append(w_sb)
 
-        cos_sb = const.tile([P, TILES, D], BF16, name="cos_sb")
-        sin_sb = const.tile([P, TILES, D], BF16, name="sin_sb")
         x_sb = {}
 
-        def load_chunk(c):
+        def load_chunk(c, pieces):
             b, cb = divmod(c, CHUNKS_PER_BATCH)
             x_sb[c] = xpool.tile([P, CHUNK * HID], BF16, name="x_c")
             rows = x[b].rearrange("(p j) k -> p (j k)", j=TILES)
-            nc.sync.dma_start(
-                out=x_sb[c][:], in_=rows[:, cb * CHUNK * HID : (cb + 1) * CHUNK * HID]
-            )
+            width = CHUNK * HID // pieces
+            for i in range(pieces):
+                nc.sync.dma_start(
+                    out=x_sb[c][:, i * width : (i + 1) * width],
+                    in_=rows[:, cb * CHUNK * HID + i * width : cb * CHUNK * HID + (i + 1) * width],
+                )
 
-        load_chunk(0)
-        load_chunk(1)
+        cos_sb = const.tile([P, TILES, D], BF16, name="cos_sb")
+        sin_sb = const.tile([P, TILES, D], BF16, name="sin_sb")
+        load_chunk(0, CHUNK)
+        load_chunk(1, 1)
         nc.sync.dma_start(out=cos_sb[:], in_=cos.rearrange("(p j) d -> p j d", j=TILES))
         nc.sync.dma_start(out=sin_sb[:], in_=sin.rearrange("(p j) d -> p j d", j=TILES))
         for c in range(2, PREFETCH):
-            load_chunk(c)
+            load_chunk(c, 1)
 
         ident = const.tile([P, P], F32, name="ident")
         masks.make_identity(nc, ident[:])
@@ -78,12 +82,12 @@ def tile_selfmha_pa_t_kernel(tc, x, Wq, Wk, Wv, cos, sin, out_0, out_1, out_2):
 
         def transpose_words(words):
             bank = psum.tile([P, WORDS], F32, name="bank", tag="bank", bufs=3)
-            for blk in range(WORDS // P):
+            for blk in range(BLOCKS):
                 cols = slice(blk * P, (blk + 1) * P)
                 nc.tensor.transpose(bank[:, cols], words[:, cols], ident[:])
             return bank
 
-        def by_pass(bank):
+        def interleaved(bank):
             return bank[:].rearrange("p (g u r) -> p g r u", g=PASSES, u=2)
 
         w_grouped = const.tile([P, 3 * PASSES * P * 4], BF16, name="w_grouped", align_bytes=64)
@@ -104,8 +108,8 @@ def tile_selfmha_pa_t_kernel(tc, x, Wq, Wk, Wv, cos, sin, out_0, out_1, out_2):
                         out=dst.rearrange("p (h i) u -> p h i u", h=HEADS), in_=halves[:, g, f]
                     )
         bank = transpose_words(w_raw[2][:].bitcast(F32))
-        nc.vector.tensor_copy(out=w_words[:, V], in_=by_pass(bank))
-        for t in range(3):
+        nc.vector.tensor_copy(out=w_words[:, V], in_=interleaved(bank))
+        for t in (LO, HI, V):
             nc.vector.quantize_mx(
                 out=w_codes[:, t * PASSES * P : (t + 1) * PASSES * P].bitcast(FP8X4),
                 scales=w_scales[:, t * PASSES * P : (t + 1) * PASSES * P],
@@ -116,8 +120,9 @@ def tile_selfmha_pa_t_kernel(tc, x, Wq, Wk, Wv, cos, sin, out_0, out_1, out_2):
         codes = {}
         scales = {}
         sums = {}
-        qk_out = {}
         rot = {}
+        qk_out = {}
+        v_out = {}
 
         def transpose_run(c, r):
             if r == 0:
@@ -129,7 +134,7 @@ def tile_selfmha_pa_t_kernel(tc, x, Wq, Wk, Wv, cos, sin, out_0, out_1, out_2):
                 bank = transpose_words(x_words[:, cols])
                 nc.scalar.copy(
                     out=g_words[:, cols].rearrange("p (g r u) -> p g r u", g=PASSES, u=2),
-                    in_=by_pass(bank),
+                    in_=interleaved(bank),
                 )
 
         def quantise_chunk(c):
@@ -150,7 +155,7 @@ def tile_selfmha_pa_t_kernel(tc, x, Wq, Wk, Wv, cos, sin, out_0, out_1, out_2):
                 vv = psum.tile([P, CHUNK * P], F32, name="vv", tag="vv", bufs=1)
                 sums[c] = (lo, hi, vv)
             for j in range(r * RUN, (r + 1) * RUN):
-                for t in range(3):
+                for t in (LO, HI, V):
                     for g in range(PASSES):
                         xc = slice((j * PASSES + g) * P, (j * PASSES + g + 1) * P)
                         wc = slice((t * PASSES + g) * P, (t * PASSES + g + 1) * P)
@@ -164,52 +169,74 @@ def tile_selfmha_pa_t_kernel(tc, x, Wq, Wk, Wv, cos, sin, out_0, out_1, out_2):
                             stop=(g == PASSES - 1),
                         )
 
-        def out_rows(out_n, c):
-            b, cb = divmod(c, CHUNKS_PER_BATCH)
-            rows = out_n[b].rearrange("h (p j) d -> p h (j d)", j=TILES)
-            return rows[:, :, cb * CHUNK * D : (cb + 1) * CHUNK * D]
+        def tiles_of(c):
+            cb = c % CHUNKS_PER_BATCH
+            return slice(cb * CHUNK, (cb + 1) * CHUNK)
 
-        def store_v(c):
-            v_out = outs.tile([P, HEADS, CHUNK, D], F32, name="v_out")
+        def store(out_n, heads, c):
+            b, cb = divmod(c, CHUNKS_PER_BATCH)
+            rows = out_n[b].rearrange("h (p j) d -> p h j d", j=TILES)
+            if b == B - 1:
+                nc.sync.dma_start(out=rows[:, :, tiles_of(c), :], in_=heads[:, :, tiles_of(c), :])
+            elif cb == CHUNKS_PER_BATCH - 1:
+                nc.sync.dma_start(out=rows, in_=heads)
+
+        def copy_and_store_v(c):
+            b, cb = divmod(c, CHUNKS_PER_BATCH)
+            if cb == 0:
+                v_out[b] = outs.tile([P, HEADS, TILES, D], F32, name="v_out")
             nc.scalar.copy(
-                out=v_out[:].rearrange("p h j d -> p j h d"),
+                out=v_out[b][:, :, tiles_of(c), :].rearrange("p h j d -> p j h d"),
                 in_=sums[c][V][:].rearrange("p (j h d) -> p j h d", j=CHUNK, h=HEADS),
             )
-            nc.sync.dma_start(out=out_rows(out_2, c), in_=v_out[:].rearrange("p h j d -> p h (j d)"))
+            store(out_2, v_out[b][:], c)
 
         def table(tab, c, f):
-            cb = c % CHUNKS_PER_BATCH
-            rows = tab[:, cb * CHUNK : (cb + 1) * CHUNK, f * HALF : (f + 1) * HALF]
+            rows = tab[:, tiles_of(c), f * HALF : (f + 1) * HALF]
             return rows.unsqueeze(2).to_broadcast([P, CHUNK, GROUPS, HALF])
 
         def rope_products(c):
-            qk_out[c] = outs.tile([P, GROUPS, CHUNK, D], F32, name="qk_out")
-            rot[c] = outs.tile([P, GROUPS, CHUNK, D], F32, name="rot")
+            b, cb = divmod(c, CHUNKS_PER_BATCH)
+            if cb == 0:
+                qk_out[b] = outs.tile([P, GROUPS, TILES, D], F32, name="qk_out")
+            rot[c] = quant.tile([P, GROUPS, CHUNK, D], F32, name="rot")
             for f in (LO, HI):
                 cols = slice(f * HALF, (f + 1) * HALF)
                 same = sums[c][f][:].rearrange("p (j g i) -> p j g i", j=CHUNK, g=GROUPS)
                 other = sums[c][1 - f][:].rearrange("p (j g i) -> p j g i", j=CHUNK, g=GROUPS)
                 nc.vector.tensor_tensor(
-                    out=qk_out[c][:, :, :, cols].rearrange("p g j i -> p j g i"),
-                    in0=same, in1=table(cos_sb, c, f), op=MULT,
+                    out=qk_out[b][:, :, tiles_of(c), cols].rearrange("p g j i -> p j g i"),
+                    in0=same,
+                    in1=table(cos_sb, c, f),
+                    op=MULT,
                 )
                 nc.vector.tensor_tensor(
                     out=rot[c][:, :, :, cols].rearrange("p g j i -> p j g i"),
-                    in0=other, in1=table(sin_sb, c, f), op=MULT,
+                    in0=other,
+                    in1=table(sin_sb, c, f),
+                    op=MULT,
                 )
 
+        def rope_sum(engine, c, groups):
+            t_cos = qk_out[c // CHUNKS_PER_BATCH][:, groups, tiles_of(c), :]
+            engine.tensor_tensor(out=t_cos, in0=t_cos, in1=rot[c][:, groups], op=ADD)
+
         def rope_sum_and_store(c):
-            adder = nc.vector if c == NCHUNKS - 1 else nc.gpsimd
-            adder.tensor_tensor(out=qk_out[c][:], in0=qk_out[c][:], in1=rot[c][:], op=ADD)
-            for n, out_n in enumerate((out_0, out_1)):
-                nc.sync.dma_start(
-                    out=out_rows(out_n, c),
-                    in_=qk_out[c][:, n * HEADS : (n + 1) * HEADS].rearrange("p h j d -> p h (j d)"),
-                )
+            qk = qk_out[c // CHUNKS_PER_BATCH]
+            q_heads, k_heads = slice(0, HEADS), slice(HEADS, GROUPS)
+            if c < NCHUNKS - 1:
+                rope_sum(nc.gpsimd, c, slice(0, GROUPS))
+                store(out_0, qk[:, q_heads], c)
+                store(out_1, qk[:, k_heads], c)
+            else:
+                rope_sum(nc.vector, c, q_heads)
+                store(out_0, qk[:, q_heads], c)
+                rope_sum(nc.vector, c, k_heads)
+                store(out_1, qk[:, k_heads], c)
 
         for s in range(-3, NCHUNKS):
             if s + 3 + PREFETCH < NCHUNKS:
-                load_chunk(s + 3 + PREFETCH)
+                load_chunk(s + 3 + PREFETCH, 1)
             if s >= 0:
                 rope_products(s)
             if 0 <= s + 2 < NCHUNKS:
@@ -220,6 +247,6 @@ def tile_selfmha_pa_t_kernel(tc, x, Wq, Wk, Wv, cos, sin, out_0, out_1, out_2):
                 if 0 <= s + 2 < NCHUNKS:
                     multiply_run(s + 2, r)
             if 0 <= s + 2 < NCHUNKS:
-                store_v(s + 2)
+                copy_and_store_v(s + 2)
             if s >= 0:
                 rope_sum_and_store(s)

@@ -24,7 +24,7 @@ BLOCKS = WORDS // P
 
 TILES = S // P
 CHUNK = 4
-RUN = 2
+RUN = 4
 RUNS = CHUNK // RUN
 CHUNKS_PER_BATCH = TILES // CHUNK
 NCHUNKS = B * CHUNKS_PER_BATCH
@@ -81,7 +81,7 @@ def tile_selfmha_pa_t_kernel(tc, x, Wq, Wk, Wv, cos, sin, out_0, out_1, out_2):
         nc.gpsimd.tensor_scalar_mul(out=sin_sb[:, :, 0:HALF], in0=sin_sb[:, :, 0:HALF], scalar1=-1.0)
 
         def transpose_words(words):
-            bank = psum.tile([P, WORDS], F32, name="bank", tag="bank", bufs=3)
+            bank = psum.tile([P, WORDS], F32, name="bank", tag="bank", bufs=4)
             for blk in range(BLOCKS):
                 cols = slice(blk * P, (blk + 1) * P)
                 nc.tensor.transpose(bank[:, cols], words[:, cols], ident[:])
@@ -152,7 +152,7 @@ def tile_selfmha_pa_t_kernel(tc, x, Wq, Wk, Wv, cos, sin, out_0, out_1, out_2):
             if r == 0:
                 lo = psum.tile([P, CHUNK * P], F32, name="lo", tag="lo", bufs=2)
                 hi = psum.tile([P, CHUNK * P], F32, name="hi", tag="hi", bufs=2)
-                vv = psum.tile([P, CHUNK * P], F32, name="vv", tag="vv", bufs=1)
+                vv = psum.tile([P, CHUNK * P], F32, name="vv", tag="bank", bufs=4)
                 sums[c] = (lo, hi, vv)
             for j in range(r * RUN, (r + 1) * RUN):
                 for t in (LO, HI, V):

from contextlib import ExitStack

import concourse.masks as masks
import concourse.mybir as mybir

F32 = mybir.dt.float32
BF16 = mybir.dt.bfloat16
U32 = mybir.dt.uint32
U8 = mybir.dt.uint8
FP8X4 = mybir.dt.float8_e4m3fn_x4
MULT = mybir.AluOpType.mult
ADD = mybir.AluOpType.add

P = 128
B, S, HID = 4, 2048, 1024
HEADS, D = 2, 64
HALF = D // 2
GROUPS = 2 * HEADS

K_PASS = 4 * P
PASSES = HID // K_PASS
WORDS = HID // 2
BLOCKS = WORDS // P

TILES = S // P
CHUNK = 4
RUN = 4
RUNS = CHUNK // RUN
CHUNKS_PER_BATCH = TILES // CHUNK
NCHUNKS = B * CHUNKS_PER_BATCH

X_BUFS = 8
PREFETCH = X_BUFS - 1
OUT_BUFS = 3

LO, HI, V = 0, 1, 2

FLOPS = 2 * B * S * HID * 3 * HEADS * D


def tile_selfmha_pa_t_kernel(tc, x, Wq, Wk, Wv, cos, sin, out_0, out_1, out_2):
    nc = tc.nc
    with ExitStack() as ctx:
        const = ctx.enter_context(tc.tile_pool(name="const", bufs=1))
        xpool = ctx.enter_context(tc.tile_pool(name="xpool", bufs=X_BUFS))
        quant = ctx.enter_context(tc.tile_pool(name="quant", bufs=3))
        outs = ctx.enter_context(tc.tile_pool(name="outs", bufs=OUT_BUFS))
        psum = ctx.enter_context(tc.psum_pool(name="psum", bufs=1))
        ctx.enter_context(tc.manual_schedule())

        w_raw = []
        for n, w in enumerate((Wq, Wk, Wv)):
            w_sb = const.tile([P, HID], BF16, name="w_raw%d" % n)
            nc.sync.dma_start(out=w_sb[:], in_=w)
            w_raw.append(w_sb)

        x_sb = {}

        def load_chunk(c, pieces):
            b, cb = divmod(c, CHUNKS_PER_BATCH)
            x_sb[c] = xpool.tile([P, CHUNK * HID], BF16, name="x_c")
            rows = x[b].rearrange("(p j) k -> p (j k)", j=TILES)
            width = CHUNK * HID // pieces
            for i in range(pieces):
                nc.sync.dma_start(
                    out=x_sb[c][:, i * width : (i + 1) * width],
                    in_=rows[:, cb * CHUNK * HID + i * width : cb * CHUNK * HID + (i + 1) * width],
                )

        cos_sb = const.tile([P, TILES, D], BF16, name="cos_sb")
        sin_sb = const.tile([P, TILES, D], BF16, name="sin_sb")
        load_chunk(0, CHUNK)
        load_chunk(1, 1)
        nc.sync.dma_start(out=cos_sb[:], in_=cos.rearrange("(p j) d -> p j d", j=TILES))
        nc.sync.dma_start(out=sin_sb[:], in_=sin.rearrange("(p j) d -> p j d", j=TILES))
        for c in range(2, PREFETCH):
            load_chunk(c, 1)

        ident = const.tile([P, P], F32, name="ident")
        masks.make_identity(nc, ident[:])
        nc.gpsimd.tensor_scalar_mul(out=sin_sb[:, :, 0:HALF], in0=sin_sb[:, :, 0:HALF], scalar1=-1.0)

        def transpose_words(words):
            bank = psum.tile([P, WORDS], F32, name="bank", tag="bank", bufs=4)
            for blk in range(BLOCKS):
                cols = slice(blk * P, (blk + 1) * P)
                nc.tensor.transpose(bank[:, cols], words[:, cols], ident[:])
            return bank

        def interleaved(bank):
            return bank[:].rearrange("p (g u r) -> p g r u", g=PASSES, u=2)

        w_grouped = const.tile([P, 3 * PASSES * P * 4], BF16, name="w_grouped", align_bytes=64)
        w_codes = const.tile([P, 3 * PASSES * P], U32, name="w_codes", align_bytes=64)
        w_scales = const.tile([P, 3 * PASSES * P], U8, name="w_scales", align_bytes=64)
        w_words = w_grouped[:].bitcast(F32).rearrange(
            "p (t g c u) -> p t g c u", t=3, g=PASSES, u=2
        )
        for n in range(2):
            bank = transpose_words(w_raw[n][:].bitcast(F32))
            halves = bank[:].rearrange(
                "p (g u h f i) -> p g f h i u", g=PASSES, u=2, h=HEADS, f=2
            )
            for g in range(PASSES):
                for f in (LO, HI):
                    dst = w_words[:, f, g, n * HEADS * HALF : (n + 1) * HEADS * HALF, :]
                    nc.vector.tensor_copy(
                        out=dst.rearrange("p (h i) u -> p h i u", h=HEADS), in_=halves[:, g, f]
                    )
        bank = transpose_words(w_raw[2][:].bitcast(F32))
        nc.vector.tensor_copy(out=w_words[:, V], in_=interleaved(bank))
        for t in (LO, HI, V):
            nc.vector.quantize_mx(
                out=w_codes[:, t * PASSES * P : (t + 1) * PASSES * P].bitcast(FP8X4),
                scales=w_scales[:, t * PASSES * P : (t + 1) * PASSES * P],
                in_=w_grouped[:, t * PASSES * P * 4 : (t + 1) * PASSES * P * 4],
            )

        grouped = {}
        codes = {}
        scales = {}
        sums = {}
        rot = {}
        qk_out = {}
        v_out = {}

        def transpose_run(c, r):
            if r == 0:
                grouped[c] = quant.tile([P, CHUNK * HID], BF16, name="grouped", align_bytes=64)
            x_words = x_sb[c][:].bitcast(F32)
            g_words = grouped[c][:].bitcast(F32)
            for j in range(r * RUN, (r + 1) * RUN):
                cols = slice(j * WORDS, (j + 1) * WORDS)
                bank = transpose_words(x_words[:, cols])
                nc.scalar.copy(
                    out=g_words[:, cols].rearrange("p (g r u) -> p g r u", g=PASSES, u=2),
                    in_=interleaved(bank),
                )

        def quantise_chunk(c):
            codes[c] = quant.tile([P, CHUNK * PASSES * P], U32, name="codes", align_bytes=64)
            scales[c] = quant.tile([P, CHUNK * PASSES * P], U8, name="scales", align_bytes=64)
            for r in range(RUNS):
                cols = slice(r * RUN * PASSES * P, (r + 1) * RUN * PASSES * P)
                nc.vector.quantize_mx(
                    out=codes[c][:, cols].bitcast(FP8X4),
                    scales=scales[c][:, cols],
                    in_=grouped[c][:, r * RUN * HID : (r + 1) * RUN * HID],
                )

        def multiply_run(c, r):
            if r == 0:
                lo = psum.tile([P, CHUNK * P], F32, name="lo", tag="lo", bufs=2)
                hi = psum.tile([P, CHUNK * P], F32, name="hi", tag="hi", bufs=2)
                vv = psum.tile([P, CHUNK * P], F32, name="vv", tag="bank", bufs=4)
                sums[c] = (lo, hi, vv)
            for j in range(r * RUN, (r + 1) * RUN):
                for t in (LO, HI, V):
                    for g in range(PASSES):
                        xc = slice((j * PASSES + g) * P, (j * PASSES + g + 1) * P)
                        wc = slice((t * PASSES + g) * P, (t * PASSES + g + 1) * P)
                        nc.tensor.matmul_mx(
                            out=sums[c][t][:, j * P : (j + 1) * P],
                            lhsT=codes[c][:, xc].bitcast(FP8X4),
                            lhsT_scale=scales[c][:, xc],
                            rhs=w_codes[:, wc].bitcast(FP8X4),
                            rhs_scale=w_scales[:, wc],
                            start=(g == 0),
                            stop=(g == PASSES - 1),
                        )

        def tiles_of(c):
            cb = c % CHUNKS_PER_BATCH
            return slice(cb * CHUNK, (cb + 1) * CHUNK)

        def store(out_n, heads, c):
            b, cb = divmod(c, CHUNKS_PER_BATCH)
            rows = out_n[b].rearrange("h (p j) d -> p h j d", j=TILES)
            if b == B - 1:
                nc.sync.dma_start(out=rows[:, :, tiles_of(c), :], in_=heads[:, :, tiles_of(c), :])
            elif cb == CHUNKS_PER_BATCH - 1:
                nc.sync.dma_start(out=rows, in_=heads)

        def copy_and_store_v(c):
            b, cb = divmod(c, CHUNKS_PER_BATCH)
            if cb == 0:
                v_out[b] = outs.tile([P, HEADS, TILES, D], F32, name="v_out")
            nc.scalar.copy(
                out=v_out[b][:, :, tiles_of(c), :].rearrange("p h j d -> p j h d"),
                in_=sums[c][V][:].rearrange("p (j h d) -> p j h d", j=CHUNK, h=HEADS),
            )
            store(out_2, v_out[b][:], c)

        def table(tab, c, f):
            rows = tab[:, tiles_of(c), f * HALF : (f + 1) * HALF]
            return rows.unsqueeze(2).to_broadcast([P, CHUNK, GROUPS, HALF])

        def rope_products(c):
            b, cb = divmod(c, CHUNKS_PER_BATCH)
            if cb == 0:
                qk_out[b] = outs.tile([P, GROUPS, TILES, D], F32, name="qk_out")
            rot[c] = quant.tile([P, GROUPS, CHUNK, D], F32, name="rot")
            for f in (LO, HI):
                cols = slice(f * HALF, (f + 1) * HALF)
                same = sums[c][f][:].rearrange("p (j g i) -> p j g i", j=CHUNK, g=GROUPS)
                other = sums[c][1 - f][:].rearrange("p (j g i) -> p j g i", j=CHUNK, g=GROUPS)
                nc.vector.tensor_tensor(
                    out=qk_out[b][:, :, tiles_of(c), cols].rearrange("p g j i -> p j g i"),
                    in0=same,
                    in1=table(cos_sb, c, f),
                    op=MULT,
                )
                nc.vector.tensor_tensor(
                    out=rot[c][:, :, :, cols].rearrange("p g j i -> p j g i"),
                    in0=other,
                    in1=table(sin_sb, c, f),
                    op=MULT,
                )

        def rope_sum(engine, c, groups):
            t_cos = qk_out[c // CHUNKS_PER_BATCH][:, groups, tiles_of(c), :]
            engine.tensor_tensor(out=t_cos, in0=t_cos, in1=rot[c][:, groups], op=ADD)

        def rope_sum_and_store(c):
            qk = qk_out[c // CHUNKS_PER_BATCH]
            q_heads, k_heads = slice(0, HEADS), slice(HEADS, GROUPS)
            if c < NCHUNKS - 1:
                rope_sum(nc.gpsimd, c, slice(0, GROUPS))
                store(out_0, qk[:, q_heads], c)
                store(out_1, qk[:, k_heads], c)
            else:
                rope_sum(nc.vector, c, q_heads)
                store(out_0, qk[:, q_heads], c)
                rope_sum(nc.vector, c, k_heads)
                store(out_1, qk[:, k_heads], c)

        for s in range(-3, NCHUNKS):
            if s + 3 + PREFETCH < NCHUNKS:
                load_chunk(s + 3 + PREFETCH, 1)
            if s >= 0:
                rope_products(s)
            if 0 <= s + 2 < NCHUNKS:
                quantise_chunk(s + 2)
            for r in range(RUNS):
                if s + 3 < NCHUNKS:
                    transpose_run(s + 3, r)
                if 0 <= s + 2 < NCHUNKS:
                    multiply_run(s + 2, r)
            if 0 <= s + 2 < NCHUNKS:
                copy_and_store_v(s + 2)
            if s >= 0:
                rope_sum_and_store(s)
